import numpy as np
import ml_dtypes

BF16 = ml_dtypes.bfloat16


def bf(x):
    return np.asarray(x, np.float32).astype(BF16)


def f32(x):
    return np.asarray(x, np.float32)


def f64(x):
    return np.asarray(x).astype(np.float64)


def striped(idx):
    return np.tile(idx.reshape(-1, 16).T, (8, 1))


C, S, N = 128, 256, 128
STEP, SHIFT, RLO, RHI, PSC = 0.1, 0.5, 0.4, 0.8, 0.25


def ball(n):
    d = np.random.standard_normal((C, n)) + SHIFT
    r = RLO + (RHI - RLO) * np.random.rand(1, n)
    return f32(r * d / np.sqrt((d * d).sum(0, keepdims=True)))


def setup_inputs():
    return {"base": ball(S), "p": ball(N), "pos": f32(PSC * (np.random.standard_normal((C, N)) + SHIFT)), "offs": striped(np.random.permutation(S)[:N])}


def reference(base, p, pos, offs):
    idx = offs[:16].T.reshape(-1)
    x = f64(p)
    u = STEP * f64(pos)
    x2 = (x * x).sum(0, keepdims=True)
    xu = (x * u).sum(0, keepdims=True)
    u2 = (u * u).sum(0, keepdims=True)
    vn = np.sqrt(u2)
    t = np.tanh(vn / (1.0 - x2)) / vn
    xy = t * xu
    y2 = t * t * u2
    num = (1.0 + 2.0 * xy + y2) * x + (1.0 - x2) * t * u
    den = 1.0 + 2.0 * xy + x2 * y2
    out = f64(base).copy()
    out[:, idx] = num * (1.0 / den)
    return out

@@ -1,0 +1,92 @@
+import concourse.mybir as mybir
+
+F32 = mybir.dt.float32
+BF16 = mybir.dt.bfloat16
+U16 = mybir.dt.uint16
+ALU = mybir.AluOpType
+ACT = mybir.ActivationFunctionType
+
+C = 128
+S = 256
+N = 128
+STEP = 0.1
+
+FLOPS = 3 * 2 * C * N
+
+
+def tile_hyperbolictransformer_kernel(tc, base, p, pos, offs, out):
+    nc = tc.nc
+    with (
+        tc.tile_pool(name="held", bufs=1) as held,
+        tc.psum_pool(name="sums", bufs=1) as sums,
+    ):
+        pos_sb = held.tile([C, N], F32)
+        p_sb = held.tile([C, N], F32)
+        window = held.tile([C, S], F32)
+        offsets = held.tile([C, N // 16], U16)
+        nc.sync.dma_start(pos_sb[:], pos)
+        nc.scalar.dma_start(p_sb[:], p)
+        nc.sync.dma_start(offsets[:], offs)
+        nc.gpsimd.dma_start(window[:], base)
+
+        ones = held.tile([C, C], BF16)
+        nc.gpsimd.memset(ones[:], 1.0)
+
+        u = held.tile([C, N], F32)
+        uu = held.tile([C, N], BF16)
+        pp = held.tile([C, N], BF16)
+        pu = held.tile([C, N], BF16)
+        nc.vector.tensor_scalar_mul(u[:], pos_sb[:], STEP)
+        nc.vector.tensor_tensor(uu[:], u[:], u[:], ALU.mult)
+        nc.vector.tensor_tensor(pp[:], p_sb[:], p_sb[:], ALU.mult)
+        nc.vector.tensor_tensor(pu[:], p_sb[:], u[:], ALU.mult)
+
+        u2 = sums.tile([C, N], F32)
+        x2 = sums.tile([C, N], F32)
+        xu = sums.tile([C, N], F32)
+        nc.tensor.matmul(u2[:], ones[:], uu[:], start=True, stop=True)
+        nc.tensor.matmul(x2[:], ones[:], pp[:], start=True, stop=True)
+        nc.tensor.matmul(xu[:], ones[:], pu[:], start=True, stop=True)
+
+        norm = held.tile([C, N], F32)
+        nc.scalar.activation(norm[:], u2[:], ACT.Sqrt)
+        gap = held.tile([C, N], F32)
+        nc.vector.tensor_scalar(gap[:], x2[:], -1.0, 1.0, ALU.mult, ALU.add)
+        inv_gap = held.tile([C, N], F32)
+        nc.vector.reciprocal(inv_gap[:], gap[:])
+        arg = held.tile([C, N], F32)
+        nc.vector.tensor_tensor(arg[:], norm[:], inv_gap[:], ALU.mult)
+        th = held.tile([C, N], F32)
+        nc.scalar.activation(th[:], arg[:], ACT.Tanh)
+        inv_norm = held.tile([C, N], F32)
+        nc.vector.reciprocal(inv_norm[:], norm[:])
+        t = held.tile([C, N], F32)
+        nc.vector.tensor_tensor(t[:], th[:], inv_norm[:], ALU.mult)
+
+        xy = held.tile([C, N], F32)
+        nc.vector.tensor_tensor(xy[:], t[:], xu[:], ALU.mult)
+        y2 = held.tile([C, N], F32)
+        nc.vector.tensor_tensor(y2[:], th[:], th[:], ALU.mult)
+        one_2xy = held.tile([C, N], F32)
+        nc.vector.tensor_scalar(one_2xy[:], xy[:], 2.0, 1.0, ALU.mult, ALU.add)
+
+        x2y2 = held.tile([C, N], F32)
+        nc.vector.tensor_tensor(x2y2[:], y2[:], x2[:], ALU.mult)
+        den = held.tile([C, N], F32)
+        nc.vector.tensor_tensor(den[:], one_2xy[:], x2y2[:], ALU.add)
+        inv_den = held.tile([C, N], F32)
+        nc.vector.reciprocal(inv_den[:], den[:])
+
+        coef_p = held.tile([C, N], F32)
+        nc.vector.tensor_tensor(coef_p[:], one_2xy[:], y2[:], ALU.add)
+        coef_u = held.tile([C, N], F32)
+        nc.vector.tensor_tensor(coef_u[:], gap[:], t[:], ALU.mult)
+        part_p = held.tile([C, N], F32)
+        nc.vector.tensor_tensor(part_p[:], coef_p[:], p_sb[:], ALU.mult)
+        part_u = held.tile([C, N], F32)
+        nc.vector.tensor_tensor(part_u[:], coef_u[:], u[:], ALU.mult)
+        num = held.tile([C, N], F32)
+        nc.vector.tensor_tensor(num[:], part_p[:], part_u[:], ALU.add)
+
+        nc.vector.tensor_tensor(window[:].indirect(offsets[:]), num[:], inv_den[:], ALU.mult)
+        nc.sync.dma_start(out, window[:])

@@ -1,4 +1,5 @@
 import concourse.mybir as mybir
+from concourse.masks import make_identity
 
 F32 = mybir.dt.float32
 BF16 = mybir.dt.bfloat16
@@ -18,7 +19,7 @@ def tile_hyperbolictransformer_kernel(tc, base, p, pos, offs, out):
     nc = tc.nc
     with (
         tc.tile_pool(name="held", bufs=1) as held,
-        tc.psum_pool(name="sums", bufs=1) as sums,
+        tc.psum_pool(name="banks", bufs=1) as banks,
     ):
         pos_sb = held.tile([C, N], F32)
         p_sb = held.tile([C, N], F32)
@@ -29,64 +30,74 @@ def tile_hyperbolictransformer_kernel(tc, base, p, pos, offs, out):
         nc.sync.dma_start(offsets[:], offs)
         nc.gpsimd.dma_start(window[:], base)
 
-        ones = held.tile([C, C], BF16)
-        nc.gpsimd.memset(ones[:], 1.0)
+        ones_col = held.tile([C, 1], BF16)
+        nc.gpsimd.memset(ones_col[:], 1.0)
+        minus_half = held.tile([N, 1], F32)
+        nc.gpsimd.memset(minus_half[:], -0.5)
+        identity = held.tile([N, N], F32)
+        make_identity(nc, identity[:])
 
-        u = held.tile([C, N], F32)
         uu = held.tile([C, N], BF16)
         pp = held.tile([C, N], BF16)
         pu = held.tile([C, N], BF16)
-        nc.vector.tensor_scalar_mul(u[:], pos_sb[:], STEP)
-        nc.vector.tensor_tensor(uu[:], u[:], u[:], ALU.mult)
+        nc.scalar.activation(uu[:], pos_sb[:], ACT.Square, scale=STEP)
         nc.vector.tensor_tensor(pp[:], p_sb[:], p_sb[:], ALU.mult)
-        nc.vector.tensor_tensor(pu[:], p_sb[:], u[:], ALU.mult)
+        nc.vector.scalar_tensor_tensor(pu[:], pos_sb[:], STEP, p_sb[:], ALU.mult, ALU.mult)
 
-        u2 = sums.tile([C, N], F32)
-        x2 = sums.tile([C, N], F32)
-        xu = sums.tile([C, N], F32)
-        nc.tensor.matmul(u2[:], ones[:], uu[:], start=True, stop=True)
-        nc.tensor.matmul(x2[:], ones[:], pp[:], start=True, stop=True)
-        nc.tensor.matmul(xu[:], ones[:], pu[:], start=True, stop=True)
+        u2_bank = banks.tile([N, 1], F32)
+        x2 = banks.tile([N, 1], F32)
+        xu = banks.tile([N, 1], F32)
+        nc.tensor.matmul(u2_bank[:], uu[:], ones_col[:], start=True, stop=True)
+        nc.tensor.matmul(x2[:], pp[:], ones_col[:], start=True, stop=True)
+        nc.tensor.matmul(xu[:], pu[:], ones_col[:], start=True, stop=True)
 
-        norm = held.tile([C, N], F32)
-        nc.scalar.activation(norm[:], u2[:], ACT.Sqrt)
-        gap = held.tile([C, N], F32)
+        u2 = held.tile([N, 1], F32)
+        nc.vector.tensor_copy(u2[:], u2_bank[:])
+        inv_norm = held.tile([N, 1], F32)
+        nc.gpsimd.tensor_tensor(inv_norm[:], u2[:], minus_half[:], ALU.pow)
+
+        gap = held.tile([N, 1], F32)
         nc.vector.tensor_scalar(gap[:], x2[:], -1.0, 1.0, ALU.mult, ALU.add)
-        inv_gap = held.tile([C, N], F32)
+        inv_gap = held.tile([N, 1], F32)
         nc.vector.reciprocal(inv_gap[:], gap[:])
-        arg = held.tile([C, N], F32)
-        nc.vector.tensor_tensor(arg[:], norm[:], inv_gap[:], ALU.mult)
-        th = held.tile([C, N], F32)
-        nc.scalar.activation(th[:], arg[:], ACT.Tanh)
-        inv_norm = held.tile([C, N], F32)
-        nc.vector.reciprocal(inv_norm[:], norm[:])
-        t = held.tile([C, N], F32)
-        nc.vector.tensor_tensor(t[:], th[:], inv_norm[:], ALU.mult)
+        u2_by_gap = held.tile([N, 1], F32)
+        nc.vector.tensor_tensor(u2_by_gap[:], u2[:], inv_gap[:], ALU.mult)
+        th = held.tile([N, 1], F32)
+        nc.scalar.activation(th[:], inv_norm[:], ACT.Tanh, scale=u2_by_gap[:])
 
-        xy = held.tile([C, N], F32)
-        nc.vector.tensor_tensor(xy[:], t[:], xu[:], ALU.mult)
-        y2 = held.tile([C, N], F32)
+        two_xu_by_norm = held.tile([N, 1], F32)
+        nc.vector.scalar_tensor_tensor(two_xu_by_norm[:], xu[:], 2.0, inv_norm[:], ALU.mult, ALU.mult)
+        gap_by_norm = held.tile([N, 1], F32)
+        nc.vector.scalar_tensor_tensor(gap_by_norm[:], gap[:], STEP, inv_norm[:], ALU.mult, ALU.mult)
+
+        y2 = held.tile([N, 1], F32)
         nc.vector.tensor_tensor(y2[:], th[:], th[:], ALU.mult)
-        one_2xy = held.tile([C, N], F32)
-        nc.vector.tensor_scalar(one_2xy[:], xy[:], 2.0, 1.0, ALU.mult, ALU.add)
-
-        x2y2 = held.tile([C, N], F32)
-        nc.vector.tensor_tensor(x2y2[:], y2[:], x2[:], ALU.mult)
-        den = held.tile([C, N], F32)
-        nc.vector.tensor_tensor(den[:], one_2xy[:], x2y2[:], ALU.add)
-        inv_den = held.tile([C, N], F32)
+        one_2xy = held.tile([N, 1], F32)
+        nc.vector.tensor_scalar(one_2xy[:], th[:], two_xu_by_norm[:], 1.0, ALU.mult, ALU.add)
+        den = held.tile([N, 1], F32)
+        nc.vector.scalar_tensor_tensor(den[:], y2[:], x2[:], one_2xy[:], ALU.mult, ALU.add)
+        inv_den = held.tile([N, 1], F32)
         nc.vector.reciprocal(inv_den[:], den[:])
-
-        coef_p = held.tile([C, N], F32)
+        coef_pos = held.tile([N, 1], F32)
+        nc.vector.tensor_tensor(coef_pos[:], th[:], gap_by_norm[:], ALU.mult)
+        coef_p = held.tile([N, 1], F32)
         nc.vector.tensor_tensor(coef_p[:], one_2xy[:], y2[:], ALU.add)
-        coef_u = held.tile([C, N], F32)
-        nc.vector.tensor_tensor(coef_u[:], gap[:], t[:], ALU.mult)
-        part_p = held.tile([C, N], F32)
-        nc.vector.tensor_tensor(part_p[:], coef_p[:], p_sb[:], ALU.mult)
-        part_u = held.tile([C, N], F32)
-        nc.vector.tensor_tensor(part_u[:], coef_u[:], u[:], ALU.mult)
-        num = held.tile([C, N], F32)
-        nc.vector.tensor_tensor(num[:], part_p[:], part_u[:], ALU.add)
 
-        nc.vector.tensor_tensor(window[:].indirect(offsets[:]), num[:], inv_den[:], ALU.mult)
+        coef_pos_rows = banks.tile([C, N], F32)
+        coef_p_rows = banks.tile([C, N], F32)
+        inv_den_bank = banks.tile([C, N], F32)
+        nc.tensor.transpose(coef_pos_rows[:], coef_pos[:].to_broadcast([N, C]), identity[:])
+        nc.tensor.transpose(coef_p_rows[:], coef_p[:].to_broadcast([N, C]), identity[:])
+        nc.tensor.transpose(inv_den_bank[:], inv_den[:].to_broadcast([N, C]), identity[:])
+
+        part_pos = held.tile([C, N], F32)
+        nc.vector.tensor_tensor(part_pos[:], coef_pos_rows[:], pos_sb[:], ALU.mult)
+        part_p = held.tile([C, N], F32)
+        nc.vector.tensor_tensor(part_p[:], coef_p_rows[:], p_sb[:], ALU.mult)
+        num = held.tile([C, N], F32)
+        nc.vector.tensor_tensor(num[:], part_p[:], part_pos[:], ALU.add)
+        inv_den_rows = held.tile([C, N], F32)
+        nc.scalar.copy(inv_den_rows[:], inv_den_bank[:])
+
+        nc.vector.tensor_tensor(window[:].indirect(offsets[:]), num[:], inv_den_rows[:], ALU.mult)
         nc.sync.dma_start(out, window[:])

@@ -40,8 +40,8 @@ def tile_hyperbolictransformer_kernel(tc, base, p, pos, offs, out):
         uu = held.tile([C, N], BF16)
         pp = held.tile([C, N], BF16)
         pu = held.tile([C, N], BF16)
-        nc.scalar.activation(uu[:], pos_sb[:], ACT.Square, scale=STEP)
-        nc.vector.tensor_tensor(pp[:], p_sb[:], p_sb[:], ALU.mult)
+        nc.vector.scalar_tensor_tensor(uu[:], pos_sb[:], STEP * STEP, pos_sb[:], ALU.mult, ALU.mult)
+        nc.scalar.activation(pp[:], p_sb[:], ACT.Square)
         nc.vector.scalar_tensor_tensor(pu[:], pos_sb[:], STEP, p_sb[:], ALU.mult, ALU.mult)
 
         u2_bank = banks.tile([N, 1], F32)
@@ -70,18 +70,18 @@ def tile_hyperbolictransformer_kernel(tc, base, p, pos, offs, out):
         gap_by_norm = held.tile([N, 1], F32)
         nc.vector.scalar_tensor_tensor(gap_by_norm[:], gap[:], STEP, inv_norm[:], ALU.mult, ALU.mult)
 
+        coef_pos = held.tile([N, 1], F32)
+        nc.vector.tensor_tensor(coef_pos[:], th[:], gap_by_norm[:], ALU.mult)
         y2 = held.tile([N, 1], F32)
         nc.vector.tensor_tensor(y2[:], th[:], th[:], ALU.mult)
         one_2xy = held.tile([N, 1], F32)
         nc.vector.tensor_scalar(one_2xy[:], th[:], two_xu_by_norm[:], 1.0, ALU.mult, ALU.add)
+        coef_p = held.tile([N, 1], F32)
+        nc.vector.tensor_tensor(coef_p[:], one_2xy[:], y2[:], ALU.add)
         den = held.tile([N, 1], F32)
         nc.vector.scalar_tensor_tensor(den[:], y2[:], x2[:], one_2xy[:], ALU.mult, ALU.add)
         inv_den = held.tile([N, 1], F32)
         nc.vector.reciprocal(inv_den[:], den[:])
-        coef_pos = held.tile([N, 1], F32)
-        nc.vector.tensor_tensor(coef_pos[:], th[:], gap_by_norm[:], ALU.mult)
-        coef_p = held.tile([N, 1], F32)
-        nc.vector.tensor_tensor(coef_p[:], one_2xy[:], y2[:], ALU.add)
 
         coef_pos_rows = banks.tile([C, N], F32)
         coef_p_rows = banks.tile([C, N], F32)

@@ -34,6 +34,8 @@ def tile_hyperbolictransformer_kernel(tc, base, p, pos, offs, out):
         nc.gpsimd.memset(ones_col[:], 1.0)
         minus_half = held.tile([N, 1], F32)
         nc.gpsimd.memset(minus_half[:], -0.5)
+        horner_adds = held.tile([N, 2], F32)
+        nc.gpsimd.memset(horner_adds[:], 1.0)
         identity = held.tile([N, N], F32)
         make_identity(nc, identity[:])
 
@@ -45,10 +47,10 @@ def tile_hyperbolictransformer_kernel(tc, base, p, pos, offs, out):
         nc.vector.scalar_tensor_tensor(pu[:], pos_sb[:], STEP, p_sb[:], ALU.mult, ALU.mult)
 
         u2_bank = banks.tile([N, 1], F32)
-        x2 = banks.tile([N, 1], F32)
+        x2_bank = banks.tile([N, 1], F32)
         xu = banks.tile([N, 1], F32)
         nc.tensor.matmul(u2_bank[:], uu[:], ones_col[:], start=True, stop=True)
-        nc.tensor.matmul(x2[:], pp[:], ones_col[:], start=True, stop=True)
+        nc.tensor.matmul(x2_bank[:], pp[:], ones_col[:], start=True, stop=True)
         nc.tensor.matmul(xu[:], pu[:], ones_col[:], start=True, stop=True)
 
         u2 = held.tile([N, 1], F32)
@@ -57,37 +59,34 @@ def tile_hyperbolictransformer_kernel(tc, base, p, pos, offs, out):
         nc.gpsimd.tensor_tensor(inv_norm[:], u2[:], minus_half[:], ALU.pow)
 
         gap = held.tile([N, 1], F32)
-        nc.vector.tensor_scalar(gap[:], x2[:], -1.0, 1.0, ALU.mult, ALU.add)
+        nc.vector.tensor_scalar(gap[:], x2_bank[:], -1.0, 1.0, ALU.mult, ALU.add)
         inv_gap = held.tile([N, 1], F32)
         nc.vector.reciprocal(inv_gap[:], gap[:])
         u2_by_gap = held.tile([N, 1], F32)
         nc.vector.tensor_tensor(u2_by_gap[:], u2[:], inv_gap[:], ALU.mult)
+        x2 = held.tile([N, 1], F32)
+        nc.vector.tensor_copy(x2[:], x2_bank[:])
         th = held.tile([N, 1], F32)
         nc.scalar.activation(th[:], inv_norm[:], ACT.Tanh, scale=u2_by_gap[:])
 
-        two_xu_by_norm = held.tile([N, 1], F32)
-        nc.vector.scalar_tensor_tensor(two_xu_by_norm[:], xu[:], 2.0, inv_norm[:], ALU.mult, ALU.mult)
+        nc.vector.scalar_tensor_tensor(horner_adds[:, 0:1], xu[:], 2.0, inv_norm[:], ALU.mult, ALU.mult)
         gap_by_norm = held.tile([N, 1], F32)
         nc.vector.scalar_tensor_tensor(gap_by_norm[:], gap[:], STEP, inv_norm[:], ALU.mult, ALU.mult)
 
         coef_pos = held.tile([N, 1], F32)
         nc.vector.tensor_tensor(coef_pos[:], th[:], gap_by_norm[:], ALU.mult)
-        y2 = held.tile([N, 1], F32)
-        nc.vector.tensor_tensor(y2[:], th[:], th[:], ALU.mult)
-        one_2xy = held.tile([N, 1], F32)
-        nc.vector.tensor_scalar(one_2xy[:], th[:], two_xu_by_norm[:], 1.0, ALU.mult, ALU.add)
-        coef_p = held.tile([N, 1], F32)
-        nc.vector.tensor_tensor(coef_p[:], one_2xy[:], y2[:], ALU.add)
-        den = held.tile([N, 1], F32)
-        nc.vector.scalar_tensor_tensor(den[:], y2[:], x2[:], one_2xy[:], ALU.mult, ALU.add)
+        coef_p_steps = held.tile([N, 2], F32)
+        nc.vector.tensor_tensor_scan(coef_p_steps[:], th[:].to_broadcast([N, 2]), horner_adds[:], 1.0, ALU.mult, ALU.add)
+        den_steps = held.tile([N, 2], F32)
+        nc.vector.tensor_tensor_scan(den_steps[:], th[:].to_broadcast([N, 2]), horner_adds[:], x2[:], ALU.mult, ALU.add)
         inv_den = held.tile([N, 1], F32)
-        nc.vector.reciprocal(inv_den[:], den[:])
+        nc.vector.reciprocal(inv_den[:], den_steps[:, 1:2])
 
         coef_pos_rows = banks.tile([C, N], F32)
         coef_p_rows = banks.tile([C, N], F32)
         inv_den_bank = banks.tile([C, N], F32)
         nc.tensor.transpose(coef_pos_rows[:], coef_pos[:].to_broadcast([N, C]), identity[:])
-        nc.tensor.transpose(coef_p_rows[:], coef_p[:].to_broadcast([N, C]), identity[:])
+        nc.tensor.transpose(coef_p_rows[:], coef_p_steps[:, 1:2].to_broadcast([N, C]), identity[:])
         nc.tensor.transpose(inv_den_bank[:], inv_den[:].to_broadcast([N, C]), identity[:])
 
         part_pos = held.tile([C, N], F32)

@@ -28,7 +28,7 @@ def tile_hyperbolictransformer_kernel(tc, base, p, pos, offs, out):
         nc.sync.dma_start(pos_sb[:], pos)
         nc.scalar.dma_start(p_sb[:], p)
         nc.sync.dma_start(offsets[:], offs)
-        nc.gpsimd.dma_start(window[:], base)
+        nc.sync.dma_start(window[:], base)
 
         ones_col = held.tile([C, 1], BF16)
         nc.gpsimd.memset(ones_col[:], 1.0)

@@ -32,8 +32,8 @@ def tile_hyperbolictransformer_kernel(tc, base, p, pos, offs, out):
 
         ones_col = held.tile([C, 1], BF16)
         nc.gpsimd.memset(ones_col[:], 1.0)
-        minus_half = held.tile([N, 1], F32)
-        nc.gpsimd.memset(minus_half[:], -0.5)
+        half = held.tile([N, 1], F32)
+        nc.gpsimd.memset(half[:], 0.5)
         horner_adds = held.tile([N, 2], F32)
         nc.gpsimd.memset(horner_adds[:], 1.0)
         identity = held.tile([N, N], F32)
@@ -55,23 +55,27 @@ def tile_hyperbolictransformer_kernel(tc, base, p, pos, offs, out):
 
         u2 = held.tile([N, 1], F32)
         nc.vector.tensor_copy(u2[:], u2_bank[:])
-        inv_norm = held.tile([N, 1], F32)
-        nc.gpsimd.tensor_tensor(inv_norm[:], u2[:], minus_half[:], ALU.pow)
+        norm = held.tile([N, 1], F32)
+        nc.gpsimd.tensor_tensor(norm[:], u2[:], half[:], ALU.pow)
 
         gap = held.tile([N, 1], F32)
         nc.vector.tensor_scalar(gap[:], x2_bank[:], -1.0, 1.0, ALU.mult, ALU.add)
         inv_gap = held.tile([N, 1], F32)
         nc.vector.reciprocal(inv_gap[:], gap[:])
-        u2_by_gap = held.tile([N, 1], F32)
-        nc.vector.tensor_tensor(u2_by_gap[:], u2[:], inv_gap[:], ALU.mult)
+        th = held.tile([N, 1], F32)
+        nc.scalar.activation(th[:], norm[:], ACT.Tanh, scale=inv_gap[:])
+
+        inv_u2 = held.tile([N, 1], F32)
+        nc.vector.reciprocal(inv_u2[:], u2_bank[:])
         x2 = held.tile([N, 1], F32)
         nc.vector.tensor_copy(x2[:], x2_bank[:])
-        th = held.tile([N, 1], F32)
-        nc.scalar.activation(th[:], inv_norm[:], ACT.Tanh, scale=u2_by_gap[:])
-
-        nc.vector.scalar_tensor_tensor(horner_adds[:, 0:1], xu[:], 2.0, inv_norm[:], ALU.mult, ALU.mult)
+        two_xu_by_u2 = held.tile([N, 1], F32)
+        nc.vector.scalar_tensor_tensor(two_xu_by_u2[:], xu[:], 2.0, inv_u2[:], ALU.mult, ALU.mult)
+        gap_by_u2 = held.tile([N, 1], F32)
+        nc.vector.scalar_tensor_tensor(gap_by_u2[:], gap[:], STEP, inv_u2[:], ALU.mult, ALU.mult)
+        nc.vector.tensor_tensor(horner_adds[:, 0:1], two_xu_by_u2[:], norm[:], ALU.mult)
         gap_by_norm = held.tile([N, 1], F32)
-        nc.vector.scalar_tensor_tensor(gap_by_norm[:], gap[:], STEP, inv_norm[:], ALU.mult, ALU.mult)
+        nc.vector.tensor_tensor(gap_by_norm[:], gap_by_u2[:], norm[:], ALU.mult)
 
         coef_pos = held.tile([N, 1], F32)
         nc.vector.tensor_tensor(coef_pos[:], th[:], gap_by_norm[:], ALU.mult)

@@ -32,8 +32,21 @@ def tile_hyperbolictransformer_kernel(tc, base, p, pos, offs, out):
 
         ones_col = held.tile([C, 1], BF16)
         nc.gpsimd.memset(ones_col[:], 1.0)
-        half = held.tile([N, 1], F32)
-        nc.gpsimd.memset(half[:], 0.5)
+        ones_block = held.tile([C, N], BF16)
+        nc.gpsimd.memset(ones_block[:], 1.0)
+        zero_and_share = held.tile([C, 2], BF16)
+        nc.gpsimd.memset(zero_and_share[:, 0:1], 0.0)
+        nc.gpsimd.memset(zero_and_share[:, 1:2], 1.0 / C)
+        plus_and_minus = held.tile([C, 2], BF16)
+        nc.gpsimd.memset(plus_and_minus[:, 0:1], 1.0)
+        nc.gpsimd.memset(plus_and_minus[:, 1:2], -1.0)
+        p_adds = held.tile([N, 2], F32)
+        nc.gpsimd.memset(p_adds[:, 0:1], 1260.0)
+        nc.gpsimd.memset(p_adds[:, 1:2], 10395.0)
+        q_adds = held.tile([N, 3], F32)
+        nc.gpsimd.memset(q_adds[:, 0:1], 210.0)
+        nc.gpsimd.memset(q_adds[:, 1:2], 4725.0)
+        nc.gpsimd.memset(q_adds[:, 2:3], 10395.0)
         horner_adds = held.tile([N, 2], F32)
         nc.gpsimd.memset(horner_adds[:], 1.0)
         identity = held.tile([N, N], F32)
@@ -44,57 +57,52 @@ def tile_hyperbolictransformer_kernel(tc, base, p, pos, offs, out):
         pu = held.tile([C, N], BF16)
         nc.vector.scalar_tensor_tensor(uu[:], pos_sb[:], STEP * STEP, pos_sb[:], ALU.mult, ALU.mult)
         nc.scalar.activation(pp[:], p_sb[:], ACT.Square)
-        nc.vector.scalar_tensor_tensor(pu[:], pos_sb[:], STEP, p_sb[:], ALU.mult, ALU.mult)
+        nc.vector.scalar_tensor_tensor(pu[:], pos_sb[:], 2.0 * STEP, p_sb[:], ALU.mult, ALU.mult)
 
-        u2_bank = banks.tile([N, 1], F32)
-        x2_bank = banks.tile([N, 1], F32)
-        xu = banks.tile([N, 1], F32)
-        nc.tensor.matmul(u2_bank[:], uu[:], ones_col[:], start=True, stop=True)
-        nc.tensor.matmul(x2_bank[:], pp[:], ones_col[:], start=True, stop=True)
-        nc.tensor.matmul(xu[:], pu[:], ones_col[:], start=True, stop=True)
+        x2_and_gap = banks.tile([N, 2], F32)
+        u2 = banks.tile([N, 1], F32)
+        two_xu = banks.tile([N, 1], F32)
+        nc.tensor.matmul(x2_and_gap[:], ones_block[:], zero_and_share[:], start=True, stop=False)
+        nc.tensor.matmul(u2[:], uu[:], ones_col[:], start=True, stop=True)
+        nc.tensor.matmul(x2_and_gap[:], pp[:], plus_and_minus[:], start=False, stop=True)
+        nc.tensor.matmul(two_xu[:], pu[:], ones_col[:], start=True, stop=True)
+        x2 = x2_and_gap[:, 0:1]
+        gap = x2_and_gap[:, 1:2]
 
-        u2 = held.tile([N, 1], F32)
-        nc.vector.tensor_copy(u2[:], u2_bank[:])
-        norm = held.tile([N, 1], F32)
-        nc.gpsimd.tensor_tensor(norm[:], u2[:], half[:], ALU.pow)
 
-        gap = held.tile([N, 1], F32)
-        nc.vector.tensor_scalar(gap[:], x2_bank[:], -1.0, 1.0, ALU.mult, ALU.add)
         inv_gap = held.tile([N, 1], F32)
-        nc.vector.reciprocal(inv_gap[:], gap[:])
-        th = held.tile([N, 1], F32)
-        nc.scalar.activation(th[:], norm[:], ACT.Tanh, scale=inv_gap[:])
+        nc.vector.reciprocal(inv_gap[:], gap)
+        w = held.tile([N, 1], F32)
+        nc.vector.scalar_tensor_tensor(w[:], inv_gap[:], u2[:], inv_gap[:], ALU.mult, ALU.mult)
+        nc.vector.tensor_tensor(horner_adds[:, 0:1], inv_gap[:], two_xu[:], ALU.mult)
 
-        inv_u2 = held.tile([N, 1], F32)
-        nc.vector.reciprocal(inv_u2[:], u2_bank[:])
-        x2 = held.tile([N, 1], F32)
-        nc.vector.tensor_copy(x2[:], x2_bank[:])
-        two_xu_by_u2 = held.tile([N, 1], F32)
-        nc.vector.scalar_tensor_tensor(two_xu_by_u2[:], xu[:], 2.0, inv_u2[:], ALU.mult, ALU.mult)
-        gap_by_u2 = held.tile([N, 1], F32)
-        nc.vector.scalar_tensor_tensor(gap_by_u2[:], gap[:], STEP, inv_u2[:], ALU.mult, ALU.mult)
-        nc.vector.tensor_tensor(horner_adds[:, 0:1], two_xu_by_u2[:], norm[:], ALU.mult)
-        gap_by_norm = held.tile([N, 1], F32)
-        nc.vector.tensor_tensor(gap_by_norm[:], gap_by_u2[:], norm[:], ALU.mult)
+        q_steps = held.tile([N, 3], F32)
+        nc.vector.tensor_tensor_scan(q_steps[:], w[:].to_broadcast([N, 3]), q_adds[:], 1.0, ALU.mult, ALU.add)
+        p_steps = held.tile([N, 2], F32)
+        nc.vector.tensor_tensor_scan(p_steps[:], w[:].to_broadcast([N, 2]), p_adds[:], 21.0, ALU.mult, ALU.add)
+        x2w = held.tile([N, 1], F32)
+        nc.vector.tensor_scalar(x2w[:], w[:], x2, None, ALU.mult)
+        inv_q = held.tile([N, 1], F32)
+        nc.vector.reciprocal(inv_q[:], q_steps[:, 2:3])
+        r = held.tile([N, 1], F32)
+        nc.vector.tensor_tensor(r[:], p_steps[:, 1:2], inv_q[:], ALU.mult)
 
-        coef_pos = held.tile([N, 1], F32)
-        nc.vector.tensor_tensor(coef_pos[:], th[:], gap_by_norm[:], ALU.mult)
-        coef_p_steps = held.tile([N, 2], F32)
-        nc.vector.tensor_tensor_scan(coef_p_steps[:], th[:].to_broadcast([N, 2]), horner_adds[:], 1.0, ALU.mult, ALU.add)
         den_steps = held.tile([N, 2], F32)
-        nc.vector.tensor_tensor_scan(den_steps[:], th[:].to_broadcast([N, 2]), horner_adds[:], x2[:], ALU.mult, ALU.add)
+        nc.vector.tensor_tensor_scan(den_steps[:], r[:].to_broadcast([N, 2]), horner_adds[:], x2w[:], ALU.mult, ALU.add)
+        coef_p_steps = held.tile([N, 2], F32)
+        nc.vector.tensor_tensor_scan(coef_p_steps[:], r[:].to_broadcast([N, 2]), horner_adds[:], w[:], ALU.mult, ALU.add)
         inv_den = held.tile([N, 1], F32)
         nc.vector.reciprocal(inv_den[:], den_steps[:, 1:2])
 
-        coef_pos_rows = banks.tile([C, N], F32)
+        r_rows = banks.tile([C, N], F32)
         coef_p_rows = banks.tile([C, N], F32)
         inv_den_bank = banks.tile([C, N], F32)
-        nc.tensor.transpose(coef_pos_rows[:], coef_pos[:].to_broadcast([N, C]), identity[:])
+        nc.tensor.transpose(r_rows[:], r[:].to_broadcast([N, C]), identity[:])
         nc.tensor.transpose(coef_p_rows[:], coef_p_steps[:, 1:2].to_broadcast([N, C]), identity[:])
         nc.tensor.transpose(inv_den_bank[:], inv_den[:].to_broadcast([N, C]), identity[:])
 
         part_pos = held.tile([C, N], F32)
-        nc.vector.tensor_tensor(part_pos[:], coef_pos_rows[:], pos_sb[:], ALU.mult)
+        nc.vector.scalar_tensor_tensor(part_pos[:], r_rows[:], STEP, pos_sb[:], ALU.mult, ALU.mult)
         part_p = held.tile([C, N], F32)
         nc.vector.tensor_tensor(part_p[:], coef_p_rows[:], p_sb[:], ALU.mult)
         num = held.tile([C, N], F32)

@@ -14,6 +14,19 @@ STEP = 0.1
 
 FLOPS = 3 * 2 * C * N
 
+R_COEFFICIENTS = (
+    5.66866641e-05,
+    -0.000538446867,
+    0.00249627434,
+    -0.00800414337,
+    0.0214483967,
+    -0.0538479833,
+    0.133315706,
+    -0.333332321,
+    0.99999999,
+)
+DEGREE = len(R_COEFFICIENTS) - 1
+
 
 def tile_hyperbolictransformer_kernel(tc, base, p, pos, offs, out):
     nc = tc.nc
@@ -25,8 +38,8 @@ def tile_hyperbolictransformer_kernel(tc, base, p, pos, offs, out):
         p_sb = held.tile([C, N], F32)
         window = held.tile([C, S], F32)
         offsets = held.tile([C, N // 16], U16)
-        nc.sync.dma_start(pos_sb[:], pos)
-        nc.scalar.dma_start(p_sb[:], p)
+        nc.sync.dma_start(p_sb[:], p)
+        nc.scalar.dma_start(pos_sb[:], pos)
         nc.sync.dma_start(offsets[:], offs)
         nc.sync.dma_start(window[:], base)
 
@@ -40,13 +53,9 @@ def tile_hyperbolictransformer_kernel(tc, base, p, pos, offs, out):
         plus_and_minus = held.tile([C, 2], BF16)
         nc.gpsimd.memset(plus_and_minus[:, 0:1], 1.0)
         nc.gpsimd.memset(plus_and_minus[:, 1:2], -1.0)
-        p_adds = held.tile([N, 2], F32)
-        nc.gpsimd.memset(p_adds[:, 0:1], 1260.0)
-        nc.gpsimd.memset(p_adds[:, 1:2], 10395.0)
-        q_adds = held.tile([N, 3], F32)
-        nc.gpsimd.memset(q_adds[:, 0:1], 210.0)
-        nc.gpsimd.memset(q_adds[:, 1:2], 4725.0)
-        nc.gpsimd.memset(q_adds[:, 2:3], 10395.0)
+        r_adds = held.tile([N, DEGREE], F32)
+        for step in range(DEGREE):
+            nc.vector.memset(r_adds[:, step : step + 1], R_COEFFICIENTS[step + 1])
         horner_adds = held.tile([N, 2], F32)
         nc.gpsimd.memset(horner_adds[:], 1.0)
         identity = held.tile([N, N], F32)
@@ -55,16 +64,16 @@ def tile_hyperbolictransformer_kernel(tc, base, p, pos, offs, out):
         uu = held.tile([C, N], BF16)
         pp = held.tile([C, N], BF16)
         pu = held.tile([C, N], BF16)
-        nc.vector.scalar_tensor_tensor(uu[:], pos_sb[:], STEP * STEP, pos_sb[:], ALU.mult, ALU.mult)
-        nc.scalar.activation(pp[:], p_sb[:], ACT.Square)
+        nc.vector.tensor_tensor(pp[:], p_sb[:], p_sb[:], ALU.mult)
+        nc.scalar.activation(uu[:], pos_sb[:], ACT.Square, scale=STEP)
         nc.vector.scalar_tensor_tensor(pu[:], pos_sb[:], 2.0 * STEP, p_sb[:], ALU.mult, ALU.mult)
 
         x2_and_gap = banks.tile([N, 2], F32)
         u2 = banks.tile([N, 1], F32)
         two_xu = banks.tile([N, 1], F32)
         nc.tensor.matmul(x2_and_gap[:], ones_block[:], zero_and_share[:], start=True, stop=False)
-        nc.tensor.matmul(u2[:], uu[:], ones_col[:], start=True, stop=True)
         nc.tensor.matmul(x2_and_gap[:], pp[:], plus_and_minus[:], start=False, stop=True)
+        nc.tensor.matmul(u2[:], uu[:], ones_col[:], start=True, stop=True)
         nc.tensor.matmul(two_xu[:], pu[:], ones_col[:], start=True, stop=True)
         x2 = x2_and_gap[:, 0:1]
         gap = x2_and_gap[:, 1:2]
@@ -76,28 +85,23 @@ def tile_hyperbolictransformer_kernel(tc, base, p, pos, offs, out):
         nc.vector.scalar_tensor_tensor(w[:], inv_gap[:], u2[:], inv_gap[:], ALU.mult, ALU.mult)
         nc.vector.tensor_tensor(horner_adds[:, 0:1], inv_gap[:], two_xu[:], ALU.mult)
 
-        q_steps = held.tile([N, 3], F32)
-        nc.vector.tensor_tensor_scan(q_steps[:], w[:].to_broadcast([N, 3]), q_adds[:], 1.0, ALU.mult, ALU.add)
-        p_steps = held.tile([N, 2], F32)
-        nc.vector.tensor_tensor_scan(p_steps[:], w[:].to_broadcast([N, 2]), p_adds[:], 21.0, ALU.mult, ALU.add)
+        r_steps = held.tile([N, DEGREE], F32)
+        nc.vector.tensor_tensor_scan(r_steps[:], w[:].to_broadcast([N, DEGREE]), r_adds[:], R_COEFFICIENTS[0], ALU.mult, ALU.add)
+        r = r_steps[:, DEGREE - 1 : DEGREE]
         x2w = held.tile([N, 1], F32)
         nc.vector.tensor_scalar(x2w[:], w[:], x2, None, ALU.mult)
-        inv_q = held.tile([N, 1], F32)
-        nc.vector.reciprocal(inv_q[:], q_steps[:, 2:3])
-        r = held.tile([N, 1], F32)
-        nc.vector.tensor_tensor(r[:], p_steps[:, 1:2], inv_q[:], ALU.mult)
 
         den_steps = held.tile([N, 2], F32)
-        nc.vector.tensor_tensor_scan(den_steps[:], r[:].to_broadcast([N, 2]), horner_adds[:], x2w[:], ALU.mult, ALU.add)
+        nc.vector.tensor_tensor_scan(den_steps[:], r.to_broadcast([N, 2]), horner_adds[:], x2w[:], ALU.mult, ALU.add)
         coef_p_steps = held.tile([N, 2], F32)
-        nc.vector.tensor_tensor_scan(coef_p_steps[:], r[:].to_broadcast([N, 2]), horner_adds[:], w[:], ALU.mult, ALU.add)
+        nc.vector.tensor_tensor_scan(coef_p_steps[:], r.to_broadcast([N, 2]), horner_adds[:], w[:], ALU.mult, ALU.add)
         inv_den = held.tile([N, 1], F32)
         nc.vector.reciprocal(inv_den[:], den_steps[:, 1:2])
 
         r_rows = banks.tile([C, N], F32)
         coef_p_rows = banks.tile([C, N], F32)
         inv_den_bank = banks.tile([C, N], F32)
-        nc.tensor.transpose(r_rows[:], r[:].to_broadcast([N, C]), identity[:])
+        nc.tensor.transpose(r_rows[:], r.to_broadcast([N, C]), identity[:])
         nc.tensor.transpose(coef_p_rows[:], coef_p_steps[:, 1:2].to_broadcast([N, C]), identity[:])
         nc.tensor.transpose(inv_den_bank[:], inv_den[:].to_broadcast([N, C]), identity[:])
 

@@ -65,7 +65,7 @@ def tile_hyperbolictransformer_kernel(tc, base, p, pos, offs, out):
         pp = held.tile([C, N], BF16)
         pu = held.tile([C, N], BF16)
         nc.vector.tensor_tensor(pp[:], p_sb[:], p_sb[:], ALU.mult)
-        nc.scalar.activation(uu[:], pos_sb[:], ACT.Square, scale=STEP)
+        nc.vector.scalar_tensor_tensor(uu[:], pos_sb[:], STEP * STEP, pos_sb[:], ALU.mult, ALU.mult)
         nc.vector.scalar_tensor_tensor(pu[:], pos_sb[:], 2.0 * STEP, p_sb[:], ALU.mult, ALU.mult)
 
         x2_and_gap = banks.tile([N, 2], F32)
@@ -109,10 +109,10 @@ def tile_hyperbolictransformer_kernel(tc, base, p, pos, offs, out):
         nc.vector.scalar_tensor_tensor(part_pos[:], r_rows[:], STEP, pos_sb[:], ALU.mult, ALU.mult)
         part_p = held.tile([C, N], F32)
         nc.vector.tensor_tensor(part_p[:], coef_p_rows[:], p_sb[:], ALU.mult)
+        inv_den_rows = held.tile([C, N], F32)
+        nc.vector.tensor_copy(inv_den_rows[:], inv_den_bank[:])
         num = held.tile([C, N], F32)
         nc.vector.tensor_tensor(num[:], part_p[:], part_pos[:], ALU.add)
-        inv_den_rows = held.tile([C, N], F32)
-        nc.scalar.copy(inv_den_rows[:], inv_den_bank[:])
 
         nc.vector.tensor_tensor(window[:].indirect(offsets[:]), num[:], inv_den_rows[:], ALU.mult)
         nc.sync.dma_start(out, window[:])

@@ -5,7 +5,6 @@ F32 = mybir.dt.float32
 BF16 = mybir.dt.bfloat16
 U16 = mybir.dt.uint16
 ALU = mybir.AluOpType
-ACT = mybir.ActivationFunctionType
 
 C = 128
 S = 256
@@ -16,8 +15,8 @@ FLOPS = 3 * 2 * C * N
 
 R_COEFFICIENTS = (
     5.66866641e-05,
-    -0.000538446867,
-    0.00249627434,
+    -0.000538446866,
+    0.00249627433,
     -0.00800414337,
     0.0214483967,
     -0.0538479833,
@@ -25,7 +24,42 @@ R_COEFFICIENTS = (
     -0.333332321,
     0.99999999,
 )
-DEGREE = len(R_COEFFICIENTS) - 1
+R_SQUARED_COEFFICIENTS = (
+    0.000346557708,
+    -0.00317845745,
+    0.013904505,
+    -0.0405938734,
+    0.0945379814,
+    -0.1959867,
+    0.37765539,
+    -0.666659651,
+    0.999999933,
+)
+X2_CENTRE = 0.4
+INVERSE_GAP_COEFFICIENTS = (
+    766.298355,
+    459.779013,
+    143.451052,
+    86.0706312,
+    60.2229586,
+    36.1337751,
+    21.4239918,
+    12.8543951,
+    7.71609672,
+    4.62965803,
+    2.77777774,
+    1.66666664,
+)
+INVERSE_GAP_DEGREE = len(INVERSE_GAP_COEFFICIENTS) - 1
+TERMS = len(R_COEFFICIENTS)
+
+FIRST = INVERSE_GAP_DEGREE + 1
+LENGTH = FIRST + TERMS + 1
+STEPS = 2 * TERMS + 1
+
+
+def quotients(values):
+    return [value / before for value, before in zip(values, [1.0] + values[:-1])]
 
 
 def tile_hyperbolictransformer_kernel(tc, base, p, pos, offs, out):
@@ -43,66 +77,89 @@ def tile_hyperbolictransformer_kernel(tc, base, p, pos, offs, out):
         nc.sync.dma_start(offsets[:], offs)
         nc.sync.dma_start(window[:], base)
 
-        ones_col = held.tile([C, 1], BF16)
-        nc.gpsimd.memset(ones_col[:], 1.0)
-        ones_block = held.tile([C, N], BF16)
-        nc.gpsimd.memset(ones_block[:], 1.0)
-        zero_and_share = held.tile([C, 2], BF16)
-        nc.gpsimd.memset(zero_and_share[:, 0:1], 0.0)
-        nc.gpsimd.memset(zero_and_share[:, 1:2], 1.0 / C)
-        plus_and_minus = held.tile([C, 2], BF16)
-        nc.gpsimd.memset(plus_and_minus[:, 0:1], 1.0)
-        nc.gpsimd.memset(plus_and_minus[:, 1:2], -1.0)
-        r_adds = held.tile([N, DEGREE], F32)
-        for step in range(DEGREE):
-            nc.vector.memset(r_adds[:, step : step + 1], R_COEFFICIENTS[step + 1])
-        horner_adds = held.tile([N, 2], F32)
-        nc.gpsimd.memset(horner_adds[:], 1.0)
         identity = held.tile([N, N], F32)
         make_identity(nc, identity[:])
 
-        uu = held.tile([C, N], BF16)
+        pairs = list(zip(R_COEFFICIENTS, R_SQUARED_COEFFICIENTS))
+        m1_factors = [1.0] + [pairs[k][0] / pairs[k + 1][1] for k in range(TERMS - 1)] + [R_COEFFICIENTS[-1]]
+        m2_factors = [d / c for c, d in pairs]
+        m1_constants = held.tile([N, LENGTH], F32)
+        nc.vector.memset(m1_constants[:, :INVERSE_GAP_DEGREE], -X2_CENTRE)
+        nc.vector.memset(m1_constants[:, INVERSE_GAP_DEGREE:FIRST], 1.0)
+        for k, quotient in enumerate(quotients(m1_factors)):
+            nc.vector.memset(m1_constants[:, FIRST + k : FIRST + k + 1], quotient)
+        m2_constants = held.tile([N, LENGTH], F32)
+        nc.gpsimd.memset(m2_constants[:], 1.0)
+        nc.gpsimd.memset(m2_constants[:, :INVERSE_GAP_DEGREE], -X2_CENTRE)
+        nc.gpsimd.memset(m2_constants[:, INVERSE_GAP_DEGREE:FIRST], 0.0)
+        for k, quotient in enumerate(quotients(m2_factors)):
+            nc.gpsimd.memset(m2_constants[:, FIRST + k : FIRST + k + 1], quotient)
+        multiplier_adds = held.tile([N, LENGTH], F32)
+        nc.vector.memset(multiplier_adds[:], 0.0)
+        for k in range(INVERSE_GAP_DEGREE):
+            nc.vector.memset(multiplier_adds[:, k : k + 1], INVERSE_GAP_COEFFICIENTS[k + 1])
+        r_adds = held.tile([N, STEPS - 1], F32)
+        nc.vector.memset(r_adds[:], 0.0)
+        nc.vector.memset(r_adds[:, 1::2], 1.0)
+
+        ones_block = held.tile([C, N], BF16)
+        nc.gpsimd.memset(ones_block[:], 1.0)
+        take_x2 = held.tile([C, LENGTH], BF16)
+        nc.gpsimd.memset(take_x2[:], 0.0)
+        nc.gpsimd.memset(take_x2[:, :INVERSE_GAP_DEGREE], 1.0)
+        take_u2 = held.tile([C, LENGTH], BF16)
+        nc.gpsimd.memset(take_u2[:], 0.0)
+        nc.gpsimd.memset(take_u2[:, INVERSE_GAP_DEGREE:FIRST], 1.0)
+        adds_one = held.tile([C, 2 * STEPS], BF16)
+        nc.gpsimd.memset(adds_one[:], 0.0)
+        nc.gpsimd.memset(adds_one[:, 0:STEPS:2], 1.0 / C)
+        nc.gpsimd.memset(adds_one[:, 2 * STEPS - 1 : 2 * STEPS], 1.0 / C)
+        adds_x2 = held.tile([C, 2 * STEPS], BF16)
+        nc.gpsimd.memset(adds_x2[:], 0.0)
+        nc.gpsimd.memset(adds_x2[:, STEPS : 2 * STEPS - 1 : 2], 1.0)
+        adds_two_xu = held.tile([C, 2 * STEPS], BF16)
+        nc.gpsimd.memset(adds_two_xu[:], 0.0)
+        nc.gpsimd.memset(adds_two_xu[:, 1:STEPS:2], 1.0)
+        nc.gpsimd.memset(adds_two_xu[:, STEPS + 1 : 2 * STEPS : 2], 1.0)
+
         pp = held.tile([C, N], BF16)
+        uu = held.tile([C, N], BF16)
         pu = held.tile([C, N], BF16)
         nc.vector.tensor_tensor(pp[:], p_sb[:], p_sb[:], ALU.mult)
         nc.vector.scalar_tensor_tensor(uu[:], pos_sb[:], STEP * STEP, pos_sb[:], ALU.mult, ALU.mult)
         nc.vector.scalar_tensor_tensor(pu[:], pos_sb[:], 2.0 * STEP, p_sb[:], ALU.mult, ALU.mult)
 
-        x2_and_gap = banks.tile([N, 2], F32)
-        u2 = banks.tile([N, 1], F32)
-        two_xu = banks.tile([N, 1], F32)
-        nc.tensor.matmul(x2_and_gap[:], ones_block[:], zero_and_share[:], start=True, stop=False)
-        nc.tensor.matmul(x2_and_gap[:], pp[:], plus_and_minus[:], start=False, stop=True)
-        nc.tensor.matmul(u2[:], uu[:], ones_col[:], start=True, stop=True)
-        nc.tensor.matmul(two_xu[:], pu[:], ones_col[:], start=True, stop=True)
-        x2 = x2_and_gap[:, 0:1]
-        gap = x2_and_gap[:, 1:2]
+        m1_data = banks.tile([N, LENGTH], F32)
+        m2_data = banks.tile([N, LENGTH], F32)
+        adds = banks.tile([N, 2 * STEPS], F32)
+        nc.tensor.matmul(m1_data[:], identity[:], m1_constants[:], start=True, stop=False)
+        nc.tensor.matmul(m2_data[:], identity[:], m2_constants[:], start=True, stop=False)
+        nc.tensor.matmul(adds[:], ones_block[:], adds_one[:], start=True, stop=False)
+        nc.tensor.matmul(m2_data[:], pp[:], take_x2[:], start=False, stop=False)
+        nc.tensor.matmul(m1_data[:], pp[:], take_x2[:], start=False, stop=True)
+        nc.tensor.matmul(m2_data[:], uu[:], take_u2[:], start=False, stop=True)
+        nc.tensor.matmul(adds[:], pp[:], adds_x2[:], start=False, stop=False)
+        nc.tensor.matmul(adds[:], pu[:], adds_two_xu[:], start=False, stop=True)
 
+        multipliers = held.tile([N, 2 * LENGTH], F32)
+        nc.vector.tensor_tensor_scan(multipliers[:, 0::2], m1_data[:], multiplier_adds[:], INVERSE_GAP_COEFFICIENTS[0], ALU.mult, ALU.add)
+        nc.vector.tensor_tensor_scan(multipliers[:, 1::2], m2_data[:], multiplier_adds[:], INVERSE_GAP_COEFFICIENTS[0], ALU.mult, ALU.add)
+        in_turn = multipliers[:, 2 * FIRST : 2 * FIRST + STEPS]
 
-        inv_gap = held.tile([N, 1], F32)
-        nc.vector.reciprocal(inv_gap[:], gap)
-        w = held.tile([N, 1], F32)
-        nc.vector.scalar_tensor_tensor(w[:], inv_gap[:], u2[:], inv_gap[:], ALU.mult, ALU.mult)
-        nc.vector.tensor_tensor(horner_adds[:, 0:1], inv_gap[:], two_xu[:], ALU.mult)
-
-        r_steps = held.tile([N, DEGREE], F32)
-        nc.vector.tensor_tensor_scan(r_steps[:], w[:].to_broadcast([N, DEGREE]), r_adds[:], R_COEFFICIENTS[0], ALU.mult, ALU.add)
-        r = r_steps[:, DEGREE - 1 : DEGREE]
-        x2w = held.tile([N, 1], F32)
-        nc.vector.tensor_scalar(x2w[:], w[:], x2, None, ALU.mult)
-
-        den_steps = held.tile([N, 2], F32)
-        nc.vector.tensor_tensor_scan(den_steps[:], r.to_broadcast([N, 2]), horner_adds[:], x2w[:], ALU.mult, ALU.add)
-        coef_p_steps = held.tile([N, 2], F32)
-        nc.vector.tensor_tensor_scan(coef_p_steps[:], r.to_broadcast([N, 2]), horner_adds[:], w[:], ALU.mult, ALU.add)
+        r_steps = held.tile([N, STEPS - 1], F32)
+        nc.vector.tensor_tensor_scan(r_steps[:], multipliers[:, 2 * FIRST : 2 * FIRST + STEPS - 1], r_adds[:], 0.0, ALU.mult, ALU.add)
+        den_steps = held.tile([N, STEPS], F32)
+        nc.vector.tensor_tensor_scan(den_steps[:], in_turn, adds[:, STEPS:], 0.0, ALU.mult, ALU.add)
+        coef_p_steps = held.tile([N, STEPS], F32)
+        nc.vector.tensor_tensor_scan(coef_p_steps[:], in_turn, adds[:, :STEPS], 0.0, ALU.mult, ALU.add)
         inv_den = held.tile([N, 1], F32)
-        nc.vector.reciprocal(inv_den[:], den_steps[:, 1:2])
+        nc.vector.reciprocal(inv_den[:], den_steps[:, STEPS - 1 : STEPS])
 
-        r_rows = banks.tile([C, N], F32)
         coef_p_rows = banks.tile([C, N], F32)
+        r_rows = banks.tile([C, N], F32)
         inv_den_bank = banks.tile([C, N], F32)
-        nc.tensor.transpose(r_rows[:], r.to_broadcast([N, C]), identity[:])
-        nc.tensor.transpose(coef_p_rows[:], coef_p_steps[:, 1:2].to_broadcast([N, C]), identity[:])
+        nc.tensor.transpose(r_rows[:], r_steps[:, STEPS - 2 : STEPS - 1].to_broadcast([N, C]), identity[:])
+        nc.tensor.transpose(coef_p_rows[:], coef_p_steps[:, STEPS - 1 : STEPS].to_broadcast([N, C]), identity[:])
         nc.tensor.transpose(inv_den_bank[:], inv_den[:].to_broadcast([N, C]), identity[:])
 
         part_pos = held.tile([C, N], F32)

@@ -14,46 +14,31 @@ STEP = 0.1
 FLOPS = 3 * 2 * C * N
 
 R_COEFFICIENTS = (
-    5.66866641e-05,
-    -0.000538446866,
-    0.00249627433,
-    -0.00800414337,
-    0.0214483967,
-    -0.0538479833,
-    0.133315706,
-    -0.333332321,
-    0.99999999,
+    -0.000181453014,
+    0.00158179921,
+    -0.006782451,
+    0.0205423937,
+    -0.0534821347,
+    0.133242887,
+    -0.333326769,
+    0.99999992,
 )
 R_SQUARED_COEFFICIENTS = (
-    0.000346557708,
-    -0.00317845745,
-    0.013904505,
-    -0.0405938734,
-    0.0945379814,
-    -0.1959867,
-    0.37765539,
-    -0.666659651,
-    0.999999933,
+    -0.000994237801,
+    0.00830426404,
+    -0.033104061,
+    0.0889762265,
+    -0.193737173,
+    0.377206716,
+    -0.666625354,
+    0.999999498,
 )
-X2_CENTRE = 0.4
-INVERSE_GAP_COEFFICIENTS = (
-    766.298355,
-    459.779013,
-    143.451052,
-    86.0706312,
-    60.2229586,
-    36.1337751,
-    21.4239918,
-    12.8543951,
-    7.71609672,
-    4.62965803,
-    2.77777774,
-    1.66666664,
-)
-INVERSE_GAP_DEGREE = len(INVERSE_GAP_COEFFICIENTS) - 1
 TERMS = len(R_COEFFICIENTS)
 
-FIRST = INVERSE_GAP_DEGREE + 1
+SLOPE = 213 / 128
+POWERS = 17
+
+FIRST = POWERS + 1
 LENGTH = FIRST + TERMS + 1
 STEPS = 2 * TERMS + 1
 
@@ -83,44 +68,34 @@ def tile_hyperbolictransformer_kernel(tc, base, p, pos, offs, out):
         pairs = list(zip(R_COEFFICIENTS, R_SQUARED_COEFFICIENTS))
         m1_factors = [1.0] + [pairs[k][0] / pairs[k + 1][1] for k in range(TERMS - 1)] + [R_COEFFICIENTS[-1]]
         m2_factors = [d / c for c, d in pairs]
+        m1_quotients = quotients([SLOPE * factor for factor in m1_factors])
+        m2_quotients = quotients([SLOPE * factor for factor in m2_factors])
         m1_constants = held.tile([N, LENGTH], F32)
-        nc.vector.memset(m1_constants[:, :INVERSE_GAP_DEGREE], -X2_CENTRE)
-        nc.vector.memset(m1_constants[:, INVERSE_GAP_DEGREE:FIRST], 1.0)
-        for k, quotient in enumerate(quotients(m1_factors)):
+        nc.vector.memset(m1_constants[:, :POWERS], 1.0 - SLOPE)
+        nc.vector.memset(m1_constants[:, POWERS:FIRST], 1.0)
+        for k, quotient in enumerate(m1_quotients):
             nc.vector.memset(m1_constants[:, FIRST + k : FIRST + k + 1], quotient)
         m2_constants = held.tile([N, LENGTH], F32)
         nc.gpsimd.memset(m2_constants[:], 1.0)
-        nc.gpsimd.memset(m2_constants[:, :INVERSE_GAP_DEGREE], -X2_CENTRE)
-        nc.gpsimd.memset(m2_constants[:, INVERSE_GAP_DEGREE:FIRST], 0.0)
-        for k, quotient in enumerate(quotients(m2_factors)):
+        nc.gpsimd.memset(m2_constants[:, :POWERS], 1.0 - SLOPE)
+        nc.gpsimd.memset(m2_constants[:, POWERS:FIRST], 0.0)
+        for k, quotient in enumerate(m2_quotients):
             nc.gpsimd.memset(m2_constants[:, FIRST + k : FIRST + k + 1], quotient)
         multiplier_adds = held.tile([N, LENGTH], F32)
         nc.vector.memset(multiplier_adds[:], 0.0)
-        for k in range(INVERSE_GAP_DEGREE):
-            nc.vector.memset(multiplier_adds[:, k : k + 1], INVERSE_GAP_COEFFICIENTS[k + 1])
+        nc.vector.memset(multiplier_adds[:, :POWERS], 1.0)
         r_adds = held.tile([N, STEPS - 1], F32)
         nc.vector.memset(r_adds[:], 0.0)
         nc.vector.memset(r_adds[:, 1::2], 1.0)
 
         ones_block = held.tile([C, N], BF16)
         nc.gpsimd.memset(ones_block[:], 1.0)
-        take_x2 = held.tile([C, LENGTH], BF16)
-        nc.gpsimd.memset(take_x2[:], 0.0)
-        nc.gpsimd.memset(take_x2[:, :INVERSE_GAP_DEGREE], 1.0)
-        take_u2 = held.tile([C, LENGTH], BF16)
-        nc.gpsimd.memset(take_u2[:], 0.0)
-        nc.gpsimd.memset(take_u2[:, INVERSE_GAP_DEGREE:FIRST], 1.0)
+        slopes = held.tile([C, POWERS], BF16)
+        nc.gpsimd.memset(slopes[:], SLOPE)
         adds_one = held.tile([C, 2 * STEPS], BF16)
         nc.gpsimd.memset(adds_one[:], 0.0)
         nc.gpsimd.memset(adds_one[:, 0:STEPS:2], 1.0 / C)
         nc.gpsimd.memset(adds_one[:, 2 * STEPS - 1 : 2 * STEPS], 1.0 / C)
-        adds_x2 = held.tile([C, 2 * STEPS], BF16)
-        nc.gpsimd.memset(adds_x2[:], 0.0)
-        nc.gpsimd.memset(adds_x2[:, STEPS : 2 * STEPS - 1 : 2], 1.0)
-        adds_two_xu = held.tile([C, 2 * STEPS], BF16)
-        nc.gpsimd.memset(adds_two_xu[:], 0.0)
-        nc.gpsimd.memset(adds_two_xu[:, 1:STEPS:2], 1.0)
-        nc.gpsimd.memset(adds_two_xu[:, STEPS + 1 : 2 * STEPS : 2], 1.0)
 
         pp = held.tile([C, N], BF16)
         uu = held.tile([C, N], BF16)
@@ -135,15 +110,16 @@ def tile_hyperbolictransformer_kernel(tc, base, p, pos, offs, out):
         nc.tensor.matmul(m1_data[:], identity[:], m1_constants[:], start=True, stop=False)
         nc.tensor.matmul(m2_data[:], identity[:], m2_constants[:], start=True, stop=False)
         nc.tensor.matmul(adds[:], ones_block[:], adds_one[:], start=True, stop=False)
-        nc.tensor.matmul(m2_data[:], pp[:], take_x2[:], start=False, stop=False)
-        nc.tensor.matmul(m1_data[:], pp[:], take_x2[:], start=False, stop=True)
-        nc.tensor.matmul(m2_data[:], uu[:], take_u2[:], start=False, stop=True)
-        nc.tensor.matmul(adds[:], pp[:], adds_x2[:], start=False, stop=False)
-        nc.tensor.matmul(adds[:], pu[:], adds_two_xu[:], start=False, stop=True)
+        nc.tensor.matmul(m2_data[:, :POWERS], pp[:], slopes[:], start=False, stop=False)
+        nc.tensor.matmul(m1_data[:, :POWERS], pp[:], slopes[:], start=False, stop=True)
+        nc.tensor.matmul(m2_data[:, POWERS:FIRST], uu[:], ones_block[:, :1], start=False, stop=True)
+        nc.tensor.matmul(adds[:, STEPS : 2 * STEPS - 1 : 2], pp[:], ones_block[:, :TERMS], start=False, stop=False)
+        nc.tensor.matmul(adds[:, 1:STEPS:2], pu[:], ones_block[:, :TERMS], start=False, stop=False)
+        nc.tensor.matmul(adds[:, STEPS + 1 : 2 * STEPS : 2], pu[:], ones_block[:, :TERMS], start=False, stop=True)
 
         multipliers = held.tile([N, 2 * LENGTH], F32)
-        nc.vector.tensor_tensor_scan(multipliers[:, 0::2], m1_data[:], multiplier_adds[:], INVERSE_GAP_COEFFICIENTS[0], ALU.mult, ALU.add)
-        nc.vector.tensor_tensor_scan(multipliers[:, 1::2], m2_data[:], multiplier_adds[:], INVERSE_GAP_COEFFICIENTS[0], ALU.mult, ALU.add)
+        nc.vector.tensor_tensor_scan(multipliers[:, 0::2], m1_data[:], multiplier_adds[:], 1.0, ALU.mult, ALU.add)
+        nc.vector.tensor_tensor_scan(multipliers[:, 1::2], m2_data[:], multiplier_adds[:], 1.0, ALU.mult, ALU.add)
         in_turn = multipliers[:, 2 * FIRST : 2 * FIRST + STEPS]
 
         r_steps = held.tile([N, STEPS - 1], F32)

@@ -141,11 +141,14 @@ def tile_hyperbolictransformer_kernel(tc, base, p, pos, offs, out):
         part_pos = held.tile([C, N], F32)
         nc.vector.scalar_tensor_tensor(part_pos[:], r_rows[:], STEP, pos_sb[:], ALU.mult, ALU.mult)
         part_p = held.tile([C, N], F32)
-        nc.vector.tensor_tensor(part_p[:], coef_p_rows[:], p_sb[:], ALU.mult)
+        halves = (slice(0, N // 2), slice(N // 2, N))
+        for half in halves:
+            nc.vector.tensor_tensor(part_p[:, half], coef_p_rows[:, half], p_sb[:, half], ALU.mult)
         inv_den_rows = held.tile([C, N], F32)
         nc.vector.tensor_copy(inv_den_rows[:], inv_den_bank[:])
         num = held.tile([C, N], F32)
-        nc.vector.tensor_tensor(num[:], part_p[:], part_pos[:], ALU.add)
+        for half in halves:
+            nc.vector.tensor_tensor(num[:, half], part_p[:, half], part_pos[:, half], ALU.add)
 
         nc.vector.tensor_tensor(window[:].indirect(offsets[:]), num[:], inv_den_rows[:], ALU.mult)
         nc.sync.dma_start(out, window[:])

import concourse.mybir as mybir
from concourse.masks import make_identity

F32 = mybir.dt.float32
BF16 = mybir.dt.bfloat16
U16 = mybir.dt.uint16
ALU = mybir.AluOpType

C = 128
S = 256
N = 128
STEP = 0.1

FLOPS = 3 * 2 * C * N

R_COEFFICIENTS = (
    -0.000181453014,
    0.00158179921,
    -0.006782451,
    0.0205423937,
    -0.0534821347,
    0.133242887,
    -0.333326769,
    0.99999992,
)
R_SQUARED_COEFFICIENTS = (
    -0.000994237801,
    0.00830426404,
    -0.033104061,
    0.0889762265,
    -0.193737173,
    0.377206716,
    -0.666625354,
    0.999999498,
)
TERMS = len(R_COEFFICIENTS)

SLOPE = 213 / 128
POWERS = 17

FIRST = POWERS + 1
LENGTH = FIRST + TERMS + 1
STEPS = 2 * TERMS + 1


def quotients(values):
    return [value / before for value, before in zip(values, [1.0] + values[:-1])]


def tile_hyperbolictransformer_kernel(tc, base, p, pos, offs, out):
    nc = tc.nc
    with (
        tc.tile_pool(name="held", bufs=1) as held,
        tc.psum_pool(name="banks", bufs=1) as banks,
    ):
        pos_sb = held.tile([C, N], F32)
        p_sb = held.tile([C, N], F32)
        window = held.tile([C, S], F32)
        offsets = held.tile([C, N // 16], U16)
        nc.sync.dma_start(p_sb[:], p)
        nc.scalar.dma_start(pos_sb[:], pos)
        nc.sync.dma_start(offsets[:], offs)
        nc.sync.dma_start(window[:], base)

        identity = held.tile([N, N], F32)
        make_identity(nc, identity[:])

        pairs = list(zip(R_COEFFICIENTS, R_SQUARED_COEFFICIENTS))
        m1_factors = [1.0] + [pairs[k][0] / pairs[k + 1][1] for k in range(TERMS - 1)] + [R_COEFFICIENTS[-1]]
        m2_factors = [d / c for c, d in pairs]
        m1_quotients = quotients([SLOPE * factor for factor in m1_factors])
        m2_quotients = quotients([SLOPE * factor for factor in m2_factors])
        m1_constants = held.tile([N, LENGTH], F32)
        nc.vector.memset(m1_constants[:, :POWERS], 1.0 - SLOPE)
        nc.vector.memset(m1_constants[:, POWERS:FIRST], 1.0)
        for k, quotient in enumerate(m1_quotients):
            nc.vector.memset(m1_constants[:, FIRST + k : FIRST + k + 1], quotient)
        m2_constants = held.tile([N, LENGTH], F32)
        nc.gpsimd.memset(m2_constants[:], 1.0)
        nc.gpsimd.memset(m2_constants[:, :POWERS], 1.0 - SLOPE)
        nc.gpsimd.memset(m2_constants[:, POWERS:FIRST], 0.0)
        for k, quotient in enumerate(m2_quotients):
            nc.gpsimd.memset(m2_constants[:, FIRST + k : FIRST + k + 1], quotient)
        multiplier_adds = held.tile([N, LENGTH], F32)
        nc.vector.memset(multiplier_adds[:], 0.0)
        nc.vector.memset(multiplier_adds[:, :POWERS], 1.0)
        r_adds = held.tile([N, STEPS - 1], F32)
        nc.vector.memset(r_adds[:], 0.0)
        nc.vector.memset(r_adds[:, 1::2], 1.0)

        ones_block = held.tile([C, N], BF16)
        nc.gpsimd.memset(ones_block[:], 1.0)
        slopes = held.tile([C, POWERS], BF16)
        nc.gpsimd.memset(slopes[:], SLOPE)
        adds_one = held.tile([C, 2 * STEPS], BF16)
        nc.gpsimd.memset(adds_one[:], 0.0)
        nc.gpsimd.memset(adds_one[:, 0:STEPS:2], 1.0 / C)
        nc.gpsimd.memset(adds_one[:, 2 * STEPS - 1 : 2 * STEPS], 1.0 / C)

        pp = held.tile([C, N], BF16)
        uu = held.tile([C, N], BF16)
        pu = held.tile([C, N], BF16)
        nc.vector.tensor_tensor(pp[:], p_sb[:], p_sb[:], ALU.mult)
        nc.vector.scalar_tensor_tensor(uu[:], pos_sb[:], STEP * STEP, pos_sb[:], ALU.mult, ALU.mult)
        nc.vector.scalar_tensor_tensor(pu[:], pos_sb[:], 2.0 * STEP, p_sb[:], ALU.mult, ALU.mult)

        m1_data = banks.tile([N, LENGTH], F32)
        m2_data = banks.tile([N, LENGTH], F32)
        adds = banks.tile([N, 2 * STEPS], F32)
        nc.tensor.matmul(m1_data[:], identity[:], m1_constants[:], start=True, stop=False)
        nc.tensor.matmul(m2_data[:], identity[:], m2_constants[:], start=True, stop=False)
        nc.tensor.matmul(adds[:], ones_block[:], adds_one[:], start=True, stop=False)
        nc.tensor.matmul(m2_data[:, :POWERS], pp[:], slopes[:], start=False, stop=False)
        nc.tensor.matmul(m1_data[:, :POWERS], pp[:], slopes[:], start=False, stop=True)
        nc.tensor.matmul(m2_data[:, POWERS:FIRST], uu[:], ones_block[:, :1], start=False, stop=True)
        nc.tensor.matmul(adds[:, STEPS : 2 * STEPS - 1 : 2], pp[:], ones_block[:, :TERMS], start=False, stop=False)
        nc.tensor.matmul(adds[:, 1:STEPS:2], pu[:], ones_block[:, :TERMS], start=False, stop=False)
        nc.tensor.matmul(adds[:, STEPS + 1 : 2 * STEPS : 2], pu[:], ones_block[:, :TERMS], start=False, stop=True)

        multipliers = held.tile([N, 2 * LENGTH], F32)
        nc.vector.tensor_tensor_scan(multipliers[:, 0::2], m1_data[:], multiplier_adds[:], 1.0, ALU.mult, ALU.add)
        nc.vector.tensor_tensor_scan(multipliers[:, 1::2], m2_data[:], multiplier_adds[:], 1.0, ALU.mult, ALU.add)
        in_turn = multipliers[:, 2 * FIRST : 2 * FIRST + STEPS]

        r_steps = held.tile([N, STEPS - 1], F32)
        nc.vector.tensor_tensor_scan(r_steps[:], multipliers[:, 2 * FIRST : 2 * FIRST + STEPS - 1], r_adds[:], 0.0, ALU.mult, ALU.add)
        den_steps = held.tile([N, STEPS], F32)
        nc.vector.tensor_tensor_scan(den_steps[:], in_turn, adds[:, STEPS:], 0.0, ALU.mult, ALU.add)
        coef_p_steps = held.tile([N, STEPS], F32)
        nc.vector.tensor_tensor_scan(coef_p_steps[:], in_turn, adds[:, :STEPS], 0.0, ALU.mult, ALU.add)
        inv_den = held.tile([N, 1], F32)
        nc.vector.reciprocal(inv_den[:], den_steps[:, STEPS - 1 : STEPS])

        coef_p_rows = banks.tile([C, N], F32)
        r_rows = banks.tile([C, N], F32)
        inv_den_bank = banks.tile([C, N], F32)
        nc.tensor.transpose(r_rows[:], r_steps[:, STEPS - 2 : STEPS - 1].to_broadcast([N, C]), identity[:])
        nc.tensor.transpose(coef_p_rows[:], coef_p_steps[:, STEPS - 1 : STEPS].to_broadcast([N, C]), identity[:])
        nc.tensor.transpose(inv_den_bank[:], inv_den[:].to_broadcast([N, C]), identity[:])

        part_pos = held.tile([C, N], F32)
        nc.vector.scalar_tensor_tensor(part_pos[:], r_rows[:], STEP, pos_sb[:], ALU.mult, ALU.mult)
        part_p = held.tile([C, N], F32)
        halves = (slice(0, N // 2), slice(N // 2, N))
        for half in halves:
            nc.vector.tensor_tensor(part_p[:, half], coef_p_rows[:, half], p_sb[:, half], ALU.mult)
        inv_den_rows = held.tile([C, N], F32)
        nc.vector.tensor_copy(inv_den_rows[:], inv_den_bank[:])
        num = held.tile([C, N], F32)
        for half in halves:
            nc.vector.tensor_tensor(num[:, half], part_p[:, half], part_pos[:, half], ALU.add)

        nc.vector.tensor_tensor(window[:].indirect(offsets[:]), num[:], inv_den_rows[:], ALU.mult)
        nc.sync.dma_start(out, window[:])
